import numpy as np
import ml_dtypes


def mxq(x, axis, fmt="e4m3"):
    dtype, down = {"e4m3": (ml_dtypes.float8_e4m3fn, 7), "e5m2": (ml_dtypes.float8_e5m2, 14)}[fmt]
    v = np.moveaxis(np.asarray(x, np.float32).astype(ml_dtypes.bfloat16).astype(np.float64), axis, -1)
    blocks = v.reshape(v.shape[:-1] + (-1, 32))
    amax = np.abs(blocks).max(-1, keepdims=True)
    byte = np.maximum(np.where(amax > 0, np.frexp(amax)[1] - 1 + 127, 0) - down, 1)
    scale = np.exp2(byte - 127.0)
    codes = (blocks / scale).astype(np.float32).astype(dtype).astype(np.float64)
    return np.moveaxis((codes * scale).reshape(v.shape), -1, axis)


WIDE = False


def mx_kscale(k):
    if not WIDE:
        return np.ones(k)
    levels = np.array([10, -10, 5, -5, 0])
    a = np.random.permutation(np.resize(levels, k // 512 * 4)).reshape(k // 512, 4)
    idx = np.arange(k)
    return np.exp2(a[idx // 512, idx % 128 // 32])


BF16 = ml_dtypes.bfloat16


def bf(x):
    return np.asarray(x, np.float32).astype(BF16)


def f64(x):
    return np.asarray(x).astype(np.float64)


B, N, D = 4, 2, 512


def select_func(A1):
    return np.mean(np.abs(A1), axis=(-2, -1), keepdims=True) > 1.0


def reset_func(A1):
    return A1 / np.max(np.abs(A1), axis=(-2, -1), keepdims=True)


def setup_inputs():
    s = mx_kscale(D)
    c = np.exp2(np.round(np.log2(s.mean())))
    kind = np.random.permutation(np.arange(B) % 4).reshape(B, 1, 1, 1)
    large = kind < 2
    zero_bias = kind % 2 == 0
    scale = np.where(large, np.random.uniform(2.2, 3.0, (B, 1, 1, 1)), np.random.uniform(0.3, 0.6, (B, 1, 1, 1)))
    A1 = np.random.standard_normal((B, 1, D, D)) * scale
    B1 = np.random.standard_normal((B, 1, D, D)) * 0.7 * np.where(zero_bias, 0.0, 1.0)
    g = np.where(large & zero_bias, s.max() / c, 1.0)
    A2 = np.random.standard_normal((B, N, D, D)) * 1.5 / np.sqrt(D) * g * c / s[:, None]
    B2 = np.random.standard_normal((B, N, D, D))
    return {"A1_atop_B1": bf(np.concatenate([A1, B1], axis=-2) * s / c),
            "A2_atop_B2": bf(np.concatenate([A2, B2], axis=-2))}


def reference(A1_atop_B1, A2_atop_B2):
    d = D
    left = f64(A1_atop_B1)
    right = f64(A2_atop_B2)
    A1 = left[..., :d, :]
    B1 = left[..., d:, :]
    is_selected = select_func(A1)
    bias_is_unmodified = np.all(B1 == 0, axis=(-2, -1), keepdims=True)
    should_reset = is_selected & bias_is_unmodified
    A1_new = np.where(should_reset, reset_func(A1), A1)
    B1_new = np.where(should_reset, np.zeros_like(B1), B1)
    top = np.concatenate([A1_new, B1_new], axis=-2)
    A2 = right[..., :d, :]
    B2 = right[..., d:, :]
    p = mxq(top, 3, "e4m3") @ mxq(A2, 2, "e4m3")
    return np.concatenate([p[..., :d, :], p[..., d:, :] + B2], axis=-2)

@@ -1,0 +1,195 @@
+from contextlib import ExitStack
+
+import concourse.mybir as mybir
+from concourse.masks import make_identity
+
+F32 = mybir.dt.float32
+BF16 = mybir.dt.bfloat16
+U32 = mybir.dt.uint32
+I32 = mybir.dt.int32
+U8 = mybir.dt.uint8
+FP8X4 = mybir.dt.float8_e4m3fn_x4
+ALU = mybir.AluOpType
+ACT = mybir.ActivationFunctionType
+AX = mybir.AxisListType
+
+B = 4
+N = 2
+D = 512
+P = 128
+RT = D // P
+PACK = 4
+
+FLOPS = 2 * B * N * (2 * D) * D * D
+
+
+def tile_updateonrightwithselectiveresetonleft_kernel(tc, A1_atop_B1, A2_atop_B2, out):
+    nc = tc.nc
+    with ExitStack() as ctx:
+        const = ctx.enter_context(tc.tile_pool(name="const", bufs=1))
+        inp = ctx.enter_context(tc.tile_pool(name="inp", bufs=1))
+        work = ctx.enter_context(tc.tile_pool(name="work", bufs=2))
+        small = ctx.enter_context(tc.tile_pool(name="small", bufs=2))
+        keep = ctx.enter_context(tc.tile_pool(name="keep", bufs=2))
+        stage = ctx.enter_context(tc.tile_pool(name="stage", bufs=8))
+        px = ctx.enter_context(tc.psum_pool(name="px", bufs=3))
+        ps = ctx.enter_context(tc.psum_pool(name="ps", bufs=1))
+        po = ctx.enter_context(tc.psum_pool(name="po", bufs=2))
+
+        a1 = []
+        b1 = []
+        a2 = []
+        b2 = []
+        for b in range(B):
+            a1_t = inp.tile([P, RT, D], BF16, name="a1_%d" % b)
+            nc.sync.dma_start(out=a1_t[:], in_=A1_atop_B1[b, 0, 0:D, :].rearrange("(p t) c -> p t c", t=RT))
+            b1_t = inp.tile([P, RT, D], BF16, name="b1_%d" % b)
+            nc.sync.dma_start(out=b1_t[:], in_=A1_atop_B1[b, 0, D : 2 * D, :].rearrange("(p t) c -> p t c", t=RT))
+            a1.append(a1_t)
+            b1.append(b1_t)
+            a2_b = []
+            b2_b = []
+            for n in range(N):
+                a2_t = inp.tile([P, PACK, D], BF16, name="a2_%d_%d" % (b, n))
+                nc.sync.dma_start(out=a2_t[:], in_=A2_atop_B2[b, n, 0:D, :].rearrange("(p j) c -> p j c", j=PACK))
+                a2_b.append(a2_t)
+            for n in range(N):
+                b2_t = inp.tile([P, RT, D], BF16, name="b2_%d_%d" % (b, n))
+                nc.sync.dma_start(out=b2_t[:], in_=A2_atop_B2[b, n, D : 2 * D, :].rearrange("(p t) c -> p t c", t=RT))
+                b2_b.append(b2_t)
+            a2.append(a2_b)
+            b2.append(b2_b)
+
+        ident = const.tile([P, P], F32, name="ident")
+        make_identity(nc, ident[:])
+        warm = const.tile([P, 1], F32, name="warm")
+        warm_out = const.tile([P, 1], F32, name="warm_out")
+        nc.vector.memset(warm[:], 0.0)
+        nc.scalar.activation(out=warm_out[:], in_=warm[:], func=ACT.Abs)
+
+        top_codes = {}
+        a2_codes = {}
+
+        def transpose_rows(x, g):
+            words = x[:].bitcast(F32).rearrange("p t (w u) -> p t u w", u=2)
+            g_words = g[:].bitcast(F32)
+            for j in range(RT // 2):
+                xt = px.tile([P, 2, 2, P], F32, tag="xt")
+                for i in range(2):
+                    for u in range(2):
+                        nc.tensor.transpose(xt[:, i, u, :], words[:, 2 * j + i, u, :], ident[:])
+                nc.scalar.copy(
+                    out=g_words[:, 2 * j : 2 * j + 2, :, :],
+                    in_=xt[:].rearrange("p i u m -> p i m u"),
+                )
+
+        def prepare_left(b):
+            abs_a = work.tile([P, RT * D], BF16, tag="abs_a", bufs=1)
+            sum_a = small.tile([P, 1], F32, tag="sum_a")
+            nc.scalar.activation(
+                out=abs_a[:], in_=a1[b][:].rearrange("p t c -> p (t c)"), func=ACT.Abs, accum_out=sum_a[:]
+            )
+            mz = small.tile([P, 2], F32, tag="mz")
+            nc.vector.tensor_scalar(
+                out=abs_a[:], in0=abs_a[:], scalar1=1.0, scalar2=None, op0=ALU.mult, op1=ALU.max,
+                accum_out=mz[:, 0:1],
+            )
+
+            g_b = work.tile([P, RT, P, PACK], BF16, tag="g_b", align_bytes=64)
+            transpose_rows(b1[b], g_b)
+            cb = keep.tile([P, D], U32, tag="cb", align_bytes=64)
+            sb = keep.tile([P, D], U8, tag="sb", align_bytes=64)
+            nc.vector.quantize_mx(
+                out=cb[:].bitcast(FP8X4), scales=sb[:], in_=g_b[:].rearrange("p t m k -> p (t m k)")
+            )
+            g_a = work.tile([P, RT, P, PACK], BF16, tag="g_a", align_bytes=64)
+            transpose_rows(a1[b], g_a)
+
+            masked = work.tile([P, D], I32, tag="masked", bufs=1)
+            nc.vector.tensor_scalar(
+                out=masked[:], in0=cb[:].bitcast(I32), scalar1=0x7F7F7F7F, scalar2=None, op0=ALU.bitwise_and
+            )
+            nc.vector.tensor_reduce(out=mz[:, 1:2], in_=masked[:], axis=AX.X, op=ALU.max)
+
+            bc = ps.tile([P, 3, P], F32, tag="bc")
+            nc.tensor.transpose(bc[:, 0, :], sum_a[:, 0:1].to_broadcast([P, P]), ident[:])
+            nc.tensor.transpose(bc[:, 1, :], mz[:, 0:1].to_broadcast([P, P]), ident[:])
+            nc.tensor.transpose(bc[:, 2, :], mz[:, 1:2].to_broadcast([P, P]), ident[:])
+            total = small.tile([P, 1], F32, tag="total")
+            nc.vector.tensor_reduce(out=total[:], in_=bc[:, 0, :], axis=AX.X, op=ALU.add)
+            peak = small.tile([P, 2], F32, tag="peak")
+            nc.vector.tensor_reduce(out=peak[:], in_=bc[:, 1:3, :], axis=AX.X, op=ALU.max)
+            sel = small.tile([P, 1], F32, tag="sel")
+            nc.vector.scalar_tensor_tensor(
+                out=sel[:], in0=total[:], scalar=float(D * D), in1=peak[:, 0:1], op0=ALU.is_gt, op1=ALU.mult
+            )
+            res = small.tile([P, 1], F32, tag="res")
+            nc.vector.scalar_tensor_tensor(
+                out=res[:], in0=peak[:, 1:2], scalar=0.0, in1=sel[:], op0=ALU.is_le, op1=ALU.mult
+            )
+            div = small.tile([P, 1], F32, tag="div")
+            nc.vector.scalar_tensor_tensor(
+                out=div[:], in0=res[:], scalar=0.0, in1=res[:], op0=ALU.is_le, op1=ALU.add
+            )
+            fac = small.tile([P, 1], F32, tag="fac")
+            nc.vector.reciprocal(out=fac[:], in_=div[:])
+
+            g_n = work.tile([P, D * PACK], BF16, tag="g_n", align_bytes=64)
+            nc.vector.tensor_scalar(
+                out=g_n[:], in0=g_a[:].rearrange("p t m k -> p (t m k)"), scalar1=fac[:, 0:1], scalar2=None,
+                op0=ALU.mult,
+            )
+            ca = keep.tile([P, D], U32, tag="ca", align_bytes=64)
+            sa = keep.tile([P, D], U8, tag="sa", align_bytes=64)
+            nc.vector.quantize_mx(out=ca[:].bitcast(FP8X4), scales=sa[:], in_=g_n[:])
+            top_codes[b] = ((ca, sa), (cb, sb))
+
+        def prepare_right(b, n):
+            g2 = work.tile([P, D, PACK], BF16, tag="g2", bufs=3, align_bytes=64)
+            dst = g2[:].rearrange("p (c i) j -> p c j i", i=4)
+            src = a2[b][n][:].rearrange("p j (c i) -> p c j i", i=4)
+            if n == 0:
+                nc.vector.tensor_copy(out=dst, in_=src)
+            else:
+                nc.scalar.copy(out=dst, in_=src)
+            c2 = keep.tile([P, D], U32, tag="c2", bufs=4, align_bytes=64)
+            s2 = keep.tile([P, D], U8, tag="s2", bufs=4, align_bytes=64)
+            nc.vector.quantize_mx(out=c2[:].bitcast(FP8X4), scales=s2[:], in_=g2[:].rearrange("p c j -> p (c j)"))
+            a2_codes[(b, n)] = (c2, s2)
+
+        def products(b, n):
+            c2, s2 = a2_codes[(b, n)]
+            st_lo = stage.tile([P, RT, D], F32, tag="st")
+            st_up = stage.tile([P, RT, D], F32, tag="st")
+            for t in range(RT):
+                cols = slice(t * P, (t + 1) * P)
+                for h in (1, 0):
+                    codes, scales = top_codes[b][h]
+                    acc = po.tile([P, D], F32, tag="acc%d" % h)
+                    nc.tensor.matmul_mx(
+                        out=acc[:],
+                        lhsT=codes[:, cols].bitcast(FP8X4),
+                        lhsT_scale=scales[:, cols],
+                        rhs=c2[:].bitcast(FP8X4),
+                        rhs_scale=s2[:],
+                        start=True,
+                        stop=True,
+                    )
+                    if h == 1:
+                        nc.vector.tensor_tensor(out=st_lo[:, t, :], in0=acc[:], in1=b2[b][n][:, t, :], op=ALU.add)
+                    else:
+                        nc.scalar.copy(out=st_up[:, t, :], in_=acc[:])
+            nc.sync.dma_start(out=out[b, n, D : 2 * D, :].rearrange("(p t) c -> p t c", t=RT), in_=st_lo[:])
+            nc.sync.dma_start(out=out[b, n, 0:D, :].rearrange("(p t) c -> p t c", t=RT), in_=st_up[:])
+
+        prepare_left(0)
+        prepare_right(0, 0)
+        prepare_right(0, 1)
+        for b in range(B):
+            products(b, 0)
+            if b + 1 < B:
+                prepare_left(b + 1)
+            products(b, 1)
+            if b + 1 < B:
+                prepare_right(b + 1, 0)
+                prepare_right(b + 1, 1)

@@ -41,20 +41,20 @@ def tile_updateonrightwithselectiveresetonleft_kernel(tc, A1_atop_B1, A2_atop_B2
         a2 = []
         b2 = []
         for b in range(B):
-            a1_t = inp.tile([P, RT, D], BF16, name="a1_%d" % b)
+            a1_t = inp.tile([P, RT, D], BF16, name="a1_%d" % b, align_bytes=256)
             nc.sync.dma_start(out=a1_t[:], in_=A1_atop_B1[b, 0, 0:D, :].rearrange("(p t) c -> p t c", t=RT))
-            b1_t = inp.tile([P, RT, D], BF16, name="b1_%d" % b)
+            b1_t = inp.tile([P, RT, D], BF16, name="b1_%d" % b, align_bytes=256)
             nc.sync.dma_start(out=b1_t[:], in_=A1_atop_B1[b, 0, D : 2 * D, :].rearrange("(p t) c -> p t c", t=RT))
             a1.append(a1_t)
             b1.append(b1_t)
             a2_b = []
             b2_b = []
             for n in range(N):
-                a2_t = inp.tile([P, PACK, D], BF16, name="a2_%d_%d" % (b, n))
+                a2_t = inp.tile([P, PACK, D], BF16, name="a2_%d_%d" % (b, n), align_bytes=256)
                 nc.sync.dma_start(out=a2_t[:], in_=A2_atop_B2[b, n, 0:D, :].rearrange("(p j) c -> p j c", j=PACK))
                 a2_b.append(a2_t)
             for n in range(N):
-                b2_t = inp.tile([P, RT, D], BF16, name="b2_%d_%d" % (b, n))
+                b2_t = inp.tile([P, RT, D], BF16, name="b2_%d_%d" % (b, n), align_bytes=256)
                 nc.sync.dma_start(out=b2_t[:], in_=A2_atop_B2[b, n, D : 2 * D, :].rearrange("(p t) c -> p t c", t=RT))
                 b2_b.append(b2_t)
             a2.append(a2_b)
@@ -159,8 +159,8 @@ def tile_updateonrightwithselectiveresetonleft_kernel(tc, A1_atop_B1, A2_atop_B2
 
         def products(b, n):
             c2, s2 = a2_codes[(b, n)]
-            st_lo = stage.tile([P, RT, D], F32, tag="st")
-            st_up = stage.tile([P, RT, D], F32, tag="st")
+            st_lo = stage.tile([P, RT, D], F32, tag="st", align_bytes=256)
+            st_up = stage.tile([P, RT, D], F32, tag="st", align_bytes=256)
             for t in range(RT):
                 cols = slice(t * P, (t + 1) * P)
                 for h in (1, 0):

from contextlib import ExitStack

import concourse.mybir as mybir
from concourse.masks import make_identity

F32 = mybir.dt.float32
BF16 = mybir.dt.bfloat16
U32 = mybir.dt.uint32
I32 = mybir.dt.int32
U8 = mybir.dt.uint8
FP8X4 = mybir.dt.float8_e4m3fn_x4
ALU = mybir.AluOpType
ACT = mybir.ActivationFunctionType
AX = mybir.AxisListType

B = 4
N = 2
D = 512
P = 128
RT = D // P
PACK = 4

FLOPS = 2 * B * N * (2 * D) * D * D


def tile_updateonrightwithselectiveresetonleft_kernel(tc, A1_atop_B1, A2_atop_B2, out):
    nc = tc.nc
    with ExitStack() as ctx:
        const = ctx.enter_context(tc.tile_pool(name="const", bufs=1))
        inp = ctx.enter_context(tc.tile_pool(name="inp", bufs=1))
        work = ctx.enter_context(tc.tile_pool(name="work", bufs=2))
        small = ctx.enter_context(tc.tile_pool(name="small", bufs=2))
        keep = ctx.enter_context(tc.tile_pool(name="keep", bufs=2))
        stage = ctx.enter_context(tc.tile_pool(name="stage", bufs=8))
        px = ctx.enter_context(tc.psum_pool(name="px", bufs=3))
        ps = ctx.enter_context(tc.psum_pool(name="ps", bufs=1))
        po = ctx.enter_context(tc.psum_pool(name="po", bufs=2))

        a1 = []
        b1 = []
        a2 = []
        b2 = []
        for b in range(B):
            a1_t = inp.tile([P, RT, D], BF16, name="a1_%d" % b, align_bytes=256)
            nc.sync.dma_start(out=a1_t[:], in_=A1_atop_B1[b, 0, 0:D, :].rearrange("(p t) c -> p t c", t=RT))
            b1_t = inp.tile([P, RT, D], BF16, name="b1_%d" % b, align_bytes=256)
            nc.sync.dma_start(out=b1_t[:], in_=A1_atop_B1[b, 0, D : 2 * D, :].rearrange("(p t) c -> p t c", t=RT))
            a1.append(a1_t)
            b1.append(b1_t)
            a2_b = []
            b2_b = []
            for n in range(N):
                a2_t = inp.tile([P, PACK, D], BF16, name="a2_%d_%d" % (b, n), align_bytes=256)
                nc.sync.dma_start(out=a2_t[:], in_=A2_atop_B2[b, n, 0:D, :].rearrange("(p j) c -> p j c", j=PACK))
                a2_b.append(a2_t)
            for n in range(N):
                b2_t = inp.tile([P, RT, D], BF16, name="b2_%d_%d" % (b, n), align_bytes=256)
                nc.sync.dma_start(out=b2_t[:], in_=A2_atop_B2[b, n, D : 2 * D, :].rearrange("(p t) c -> p t c", t=RT))
                b2_b.append(b2_t)
            a2.append(a2_b)
            b2.append(b2_b)

        ident = const.tile([P, P], F32, name="ident")
        make_identity(nc, ident[:])
        warm = const.tile([P, 1], F32, name="warm")
        warm_out = const.tile([P, 1], F32, name="warm_out")
        nc.vector.memset(warm[:], 0.0)
        nc.scalar.activation(out=warm_out[:], in_=warm[:], func=ACT.Abs)

        top_codes = {}
        a2_codes = {}

        def transpose_rows(x, g):
            words = x[:].bitcast(F32).rearrange("p t (w u) -> p t u w", u=2)
            g_words = g[:].bitcast(F32)
            for j in range(RT // 2):
                xt = px.tile([P, 2, 2, P], F32, tag="xt")
                for i in range(2):
                    for u in range(2):
                        nc.tensor.transpose(xt[:, i, u, :], words[:, 2 * j + i, u, :], ident[:])
                nc.scalar.copy(
                    out=g_words[:, 2 * j : 2 * j + 2, :, :],
                    in_=xt[:].rearrange("p i u m -> p i m u"),
                )

        def prepare_left(b):
            abs_a = work.tile([P, RT * D], BF16, tag="abs_a", bufs=1)
            sum_a = small.tile([P, 1], F32, tag="sum_a")
            nc.scalar.activation(
                out=abs_a[:], in_=a1[b][:].rearrange("p t c -> p (t c)"), func=ACT.Abs, accum_out=sum_a[:]
            )
            mz = small.tile([P, 2], F32, tag="mz")
            nc.vector.tensor_scalar(
                out=abs_a[:], in0=abs_a[:], scalar1=1.0, scalar2=None, op0=ALU.mult, op1=ALU.max,
                accum_out=mz[:, 0:1],
            )

            g_b = work.tile([P, RT, P, PACK], BF16, tag="g_b", align_bytes=64)
            transpose_rows(b1[b], g_b)
            cb = keep.tile([P, D], U32, tag="cb", align_bytes=64)
            sb = keep.tile([P, D], U8, tag="sb", align_bytes=64)
            nc.vector.quantize_mx(
                out=cb[:].bitcast(FP8X4), scales=sb[:], in_=g_b[:].rearrange("p t m k -> p (t m k)")
            )
            g_a = work.tile([P, RT, P, PACK], BF16, tag="g_a", align_bytes=64)
            transpose_rows(a1[b], g_a)

            masked = work.tile([P, D], I32, tag="masked", bufs=1)
            nc.vector.tensor_scalar(
                out=masked[:], in0=cb[:].bitcast(I32), scalar1=0x7F7F7F7F, scalar2=None, op0=ALU.bitwise_and
            )
            nc.vector.tensor_reduce(out=mz[:, 1:2], in_=masked[:], axis=AX.X, op=ALU.max)

            bc = ps.tile([P, 3, P], F32, tag="bc")
            nc.tensor.transpose(bc[:, 0, :], sum_a[:, 0:1].to_broadcast([P, P]), ident[:])
            nc.tensor.transpose(bc[:, 1, :], mz[:, 0:1].to_broadcast([P, P]), ident[:])
            nc.tensor.transpose(bc[:, 2, :], mz[:, 1:2].to_broadcast([P, P]), ident[:])
            total = small.tile([P, 1], F32, tag="total")
            nc.vector.tensor_reduce(out=total[:], in_=bc[:, 0, :], axis=AX.X, op=ALU.add)
            peak = small.tile([P, 2], F32, tag="peak")
            nc.vector.tensor_reduce(out=peak[:], in_=bc[:, 1:3, :], axis=AX.X, op=ALU.max)
            sel = small.tile([P, 1], F32, tag="sel")
            nc.vector.scalar_tensor_tensor(
                out=sel[:], in0=total[:], scalar=float(D * D), in1=peak[:, 0:1], op0=ALU.is_gt, op1=ALU.mult
            )
            res = small.tile([P, 1], F32, tag="res")
            nc.vector.scalar_tensor_tensor(
                out=res[:], in0=peak[:, 1:2], scalar=0.0, in1=sel[:], op0=ALU.is_le, op1=ALU.mult
            )
            div = small.tile([P, 1], F32, tag="div")
            nc.vector.scalar_tensor_tensor(
                out=div[:], in0=res[:], scalar=0.0, in1=res[:], op0=ALU.is_le, op1=ALU.add
            )
            fac = small.tile([P, 1], F32, tag="fac")
            nc.vector.reciprocal(out=fac[:], in_=div[:])

            g_n = work.tile([P, D * PACK], BF16, tag="g_n", align_bytes=64)
            nc.vector.tensor_scalar(
                out=g_n[:], in0=g_a[:].rearrange("p t m k -> p (t m k)"), scalar1=fac[:, 0:1], scalar2=None,
                op0=ALU.mult,
            )
            ca = keep.tile([P, D], U32, tag="ca", align_bytes=64)
            sa = keep.tile([P, D], U8, tag="sa", align_bytes=64)
            nc.vector.quantize_mx(out=ca[:].bitcast(FP8X4), scales=sa[:], in_=g_n[:])
            top_codes[b] = ((ca, sa), (cb, sb))

        def prepare_right(b, n):
            g2 = work.tile([P, D, PACK], BF16, tag="g2", bufs=3, align_bytes=64)
            dst = g2[:].rearrange("p (c i) j -> p c j i", i=4)
            src = a2[b][n][:].rearrange("p j (c i) -> p c j i", i=4)
            if n == 0:
                nc.vector.tensor_copy(out=dst, in_=src)
            else:
                nc.scalar.copy(out=dst, in_=src)
            c2 = keep.tile([P, D], U32, tag="c2", bufs=4, align_bytes=64)
            s2 = keep.tile([P, D], U8, tag="s2", bufs=4, align_bytes=64)
            nc.vector.quantize_mx(out=c2[:].bitcast(FP8X4), scales=s2[:], in_=g2[:].rearrange("p c j -> p (c j)"))
            a2_codes[(b, n)] = (c2, s2)

        def products(b, n):
            c2, s2 = a2_codes[(b, n)]
            st_lo = stage.tile([P, RT, D], F32, tag="st", align_bytes=256)
            st_up = stage.tile([P, RT, D], F32, tag="st", align_bytes=256)
            for t in range(RT):
                cols = slice(t * P, (t + 1) * P)
                for h in (1, 0):
                    codes, scales = top_codes[b][h]
                    acc = po.tile([P, D], F32, tag="acc%d" % h)
                    nc.tensor.matmul_mx(
                        out=acc[:],
                        lhsT=codes[:, cols].bitcast(FP8X4),
                        lhsT_scale=scales[:, cols],
                        rhs=c2[:].bitcast(FP8X4),
                        rhs_scale=s2[:],
                        start=True,
                        stop=True,
                    )
                    if h == 1:
                        nc.vector.tensor_tensor(out=st_lo[:, t, :], in0=acc[:], in1=b2[b][n][:, t, :], op=ALU.add)
                    else:
                        nc.scalar.copy(out=st_up[:, t, :], in_=acc[:])
            nc.sync.dma_start(out=out[b, n, D : 2 * D, :].rearrange("(p t) c -> p t c", t=RT), in_=st_lo[:])
            nc.sync.dma_start(out=out[b, n, 0:D, :].rearrange("(p t) c -> p t c", t=RT), in_=st_up[:])

        prepare_left(0)
        prepare_right(0, 0)
        prepare_right(0, 1)
        for b in range(B):
            products(b, 0)
            if b + 1 < B:
                prepare_left(b + 1)
            products(b, 1)
            if b + 1 < B:
                prepare_right(b + 1, 0)
                prepare_right(b + 1, 1)
